import numpy as np
import ml_dtypes


def mxq(x, axis, fmt="e4m3"):
    dtype, down = {"e4m3": (ml_dtypes.float8_e4m3fn, 7), "e5m2": (ml_dtypes.float8_e5m2, 14)}[fmt]
    v = np.moveaxis(np.asarray(x, np.float32).astype(ml_dtypes.bfloat16).astype(np.float64), axis, -1)
    blocks = v.reshape(v.shape[:-1] + (-1, 32))
    amax = np.abs(blocks).max(-1, keepdims=True)
    byte = np.maximum(np.where(amax > 0, np.frexp(amax)[1] - 1 + 127, 0) - down, 1)
    scale = np.exp2(byte - 127.0)
    codes = (blocks / scale).astype(np.float32).astype(dtype).astype(np.float64)
    return np.moveaxis((codes * scale).reshape(v.shape), -1, axis)


WIDE = False


def mx_kscale(k):
    if not WIDE:
        return np.ones(k)
    levels = np.array([30, -30])
    if k % 512:
        return np.exp2(np.random.permutation(np.resize(levels, k // 32))).repeat(32)
    a = np.empty((k // 512, 16))
    for p in range(k // 512):
        a[p, :8] = np.random.permutation(np.resize(levels, 8))
        for g in range(8):
            far = levels[np.abs(levels - a[p, g]) >= 10]
            a[p, g + 8] = far[np.random.randint(len(far))]
    return np.exp2(a.ravel()).repeat(32)


BF16 = ml_dtypes.bfloat16


def bf(x):
    return np.asarray(x, np.float32).astype(BF16)


def f64(x):
    return np.asarray(x).astype(np.float64)


B, C, H, W = 2, 512, 16, 512

TEMPERATURE = 1.0
DISP_CLAMP = 0.1
SIG = np.sqrt(2.0)


def setup_inputs():
    s = mx_kscale(C)[None, :, None, None]
    return {"img1": bf(np.random.standard_normal((B, C, H, W)) * SIG * s),
            "img2": bf(np.random.standard_normal((B, C, H, W)) * SIG / s),
            "intri1": bf(np.random.uniform(0.5, 1.5, (B, 3, 3))),
            "intri2": bf(np.random.uniform(0.5, 1.5, (B, 3, 3))),
            "extri1": bf(np.random.uniform(0.0, 1.0, (B, 4, 4))),
            "extri2": bf(np.random.uniform(0.5, 1.5, (B, 4, 4)))}


def reference(img1, img2, intri1, intri2, extri1, extri2):
    a = mxq(f64(img1), 1, "e5m2").transpose(0, 2, 3, 1)
    b = mxq(f64(img2), 1, "e5m2").transpose(0, 2, 1, 3)
    vol = (a @ b) / np.sqrt(C)
    idx = np.arange(W) * 1.0
    tril = np.where(idx[None, :] <= idx[:, None], 1.0, 0.0)
    z = vol / TEMPERATURE
    e = np.exp(z - z.max(-1, keepdims=True))
    prob = e / e.sum(-1, keepdims=True) * tril
    corresp = np.sum(prob * idx, axis=-1)[:, None]
    confidence = np.max(prob, axis=-1)[:, None]
    disp = np.abs(corresp - idx) / W
    disp = np.maximum(disp, DISP_CLAMP)
    fx = f64(intri1)[:, 0, 0][:, None, None, None]
    d = f64(extri1)[:, :3, 3] - f64(extri2)[:, :3, 3]
    baseline = np.sqrt(np.sum(d * d, axis=-1))[:, None, None, None]
    depth = fx * baseline / disp
    return depth, confidence

@@ -1,0 +1,327 @@
+import math
+from contextlib import ExitStack
+
+import concourse.mybir as mybir
+from concourse.masks import make_identity
+
+B, C, H, W = 2, 512, 16, 512
+FLOPS = 2 * B * H * W * W * C
+
+F32 = mybir.dt.float32
+BF16 = mybir.dt.bfloat16
+U32 = mybir.dt.uint32
+U8 = mybir.dt.uint8
+E5M2X4 = mybir.dt.float8_e5m2_x4
+ALU = mybir.AluOpType
+ACT = mybir.ActivationFunctionType
+AX = mybir.AxisListType
+
+P = 128
+PACK = 4
+ROWS = B * H
+TILES = W // P
+SCALE = 1.0 / math.sqrt(C)
+DISP_CLAMP = 0.1
+E_PITCH = W + P
+
+SHARE_A = (0, 320)
+SHARE_B = (320, 640)
+SHARE_G = (640, 1024)
+
+
+def tile_costvolume_kernel(tc, img1, img2, intri1, intri2, extri1, extri2, out_0, out_1):
+    nc = tc.nc
+    with ExitStack() as ctx:
+        const = ctx.enter_context(tc.tile_pool(name="const", bufs=1))
+        raw_pool = ctx.enter_context(tc.tile_pool(name="raw", bufs=4))
+        grouped_pool = ctx.enter_context(tc.tile_pool(name="grouped", bufs=3))
+        code_pool = ctx.enter_context(tc.tile_pool(name="codes", bufs=3))
+        e_pool = ctx.enter_context(tc.tile_pool(name="e", bufs=3))
+        prod_pool = ctx.enter_context(tc.tile_pool(name="prod", bufs=3))
+        fin_pool = ctx.enter_context(tc.tile_pool(name="fin", bufs=2))
+        vol_pool = ctx.enter_context(tc.psum_pool(name="vol", bufs=6))
+        psum_const = ctx.enter_context(tc.psum_pool(name="psum_const", bufs=1))
+        ctx.enter_context(tc.manual_schedule())
+
+        block_max = const.tile([P, ROWS, TILES, TILES], F32, name="block_max")
+        row_max = const.tile([P, ROWS, TILES], F32, name="row_max")
+        bias = const.tile([P, ROWS, TILES], F32, name="bias")
+        e_sum = const.tile([P, ROWS, TILES], F32, name="e_sum")
+        idx_sum = const.tile([P, ROWS, TILES], F32, name="idx_sum")
+        e_max = const.tile([P, ROWS, TILES], F32, name="e_max")
+        ident = const.tile([P, P], F32, name="ident")
+        w_col = const.tile([P, TILES, P], F32, name="w_col")
+        w1_table = const.tile([P, H, TILES], F32, name="w1_table")
+        half = const.tile([P, B], F32, name="half")
+        ramp = psum_const.tile([P, W], F32, name="ramp")
+
+        raws, groups, codes, scales, es, vols = {}, {}, {}, {}, {}, {}
+        side_steps = []
+
+        def vec():
+            if side_steps:
+                side_steps.pop(0)()
+            return nc.vector
+
+        def load(n):
+            if n >= ROWS:
+                return
+            b, h = divmod(n, H)
+            raws[n] = raw_pool.tile([P, PACK, 2 * W], BF16, name="raw")
+            for k, img in enumerate((img1, img2)):
+                nc.sync.dma_start(
+                    out=raws[n][:, :, k * W : (k + 1) * W],
+                    in_=img[b, :, h, :].rearrange("(p j) w -> p j w", j=PACK),
+                )
+
+        def interleave(engine, n, share):
+            if n >= ROWS:
+                return
+            if n not in groups:
+                groups[n] = grouped_pool.tile([P, 2 * W, PACK], BF16, name="grouped", align_bytes=64)
+            lo, hi = share
+            dst = groups[n][:, lo:hi, :]
+            src = raws[n][:, :, lo:hi]
+            if engine == "gpsimd":
+                nc.gpsimd.tensor_copy(out=dst, in_=src.rearrange("p t w -> p w t"))
+                return
+            dst = dst.rearrange("p (c i) t -> p c t i", i=4)
+            src = src.rearrange("p t (c i) -> p c t i", i=4)
+            if engine == "scalar":
+                nc.scalar.copy(out=dst, in_=src)
+            else:
+                nc.vector.tensor_copy(out=dst, in_=src)
+
+        def quantize(n):
+            if n >= ROWS:
+                return
+            codes[n] = code_pool.tile([P, 2 * W], U32, name="code", align_bytes=64)
+            scales[n] = code_pool.tile([P, 2 * W], U8, name="scale", align_bytes=64)
+            vec().quantize_mx(
+                out=codes[n][:].bitcast(E5M2X4),
+                scales=scales[n][:],
+                in_=groups[n][:].rearrange("p w t -> p (w t)"),
+            )
+
+        def correlate(n, i):
+            vols[n, i] = vol_pool.tile([P, W], F32, name="vol")
+            nc.tensor.matmul_mx(
+                out=vols[n, i][:],
+                lhsT=codes[n][:, i * P : (i + 1) * P].bitcast(E5M2X4),
+                lhsT_scale=scales[n][:, i * P : (i + 1) * P],
+                rhs=codes[n][:, W : 2 * W].bitcast(E5M2X4),
+                rhs_scale=scales[n][:, W : 2 * W],
+                start=True,
+                stop=True,
+            )
+
+        def block_maxima(n, i):
+            vec().tensor_reduce(
+                out=block_max[:, n, i, :],
+                in_=vols[n, i][:].rearrange("p (j c) -> p j c", c=P),
+                axis=AX.X,
+                op=ALU.max,
+            )
+
+        def diagonals(n, first, count):
+            return es[n][:].rearrange("p (i c) -> p i c", c=E_PITCH)[:, first : first + count, 0:P]
+
+        def softmax_pair(n, first):
+            pair = slice(first, first + 2)
+            vec().tensor_reduce(out=row_max[:, n, pair], in_=block_max[:, n, pair, :], axis=AX.X, op=ALU.max)
+            nc.scalar.activation(out=bias[:, n, pair], in_=row_max[:, n, pair], func=ACT.Copy, scale=-SCALE)
+            if n not in es:
+                es[n] = e_pool.tile([P, TILES * E_PITCH], F32, name="e")
+            for i in (first, first + 1):
+                nc.scalar.activation(
+                    out=es[n][:, i * W : (i + 1) * W],
+                    in_=vols[n, i][:],
+                    func=ACT.Exp,
+                    scale=SCALE,
+                    bias=bias[:, n, i : i + 1],
+                    accum_out=e_sum[:, n, i : i + 1],
+                )
+            nc.gpsimd.affine_select(
+                out=diagonals(n, first, 2),
+                in_=diagonals(n, first, 2),
+                pattern=[[0, 2], [-1, P]],
+                compare_op=ALU.is_ge,
+                fill=0.0,
+                base=0,
+                channel_multiplier=1,
+            )
+
+        def index_sum(n, i):
+            if n < 0:
+                return
+            width = (i + 1) * P
+            prod = prod_pool.tile([P, W], F32, name="prod")
+            vec().scalar_tensor_tensor(
+                out=prod[:, 0:width],
+                in0=es[n][:, i * W : i * W + width],
+                scalar=1.0,
+                in1=ramp[:, 0:width],
+                op0=ALU.mult,
+                op1=ALU.mult,
+                accum_out=idx_sum[:, n, i : i + 1],
+            )
+
+        def diagonal_max(n):
+            if n < 0:
+                return
+            vec().tensor_reduce(out=e_max[:, n, :], in_=diagonals(n, 0, TILES), axis=AX.X, op=ALU.max)
+
+        focal_base = const.tile([P, B], F32, name="focal_base")
+
+        def camera_steps():
+            k1 = const.tile([P, B * 9], BF16, name="k1")
+            x1 = const.tile([P, B * 16], BF16, name="x1")
+            x2 = const.tile([P, B * 16], BF16, name="x2")
+            nc.sync.dma_start(out=k1[:], in_=intri1.rearrange("b r c -> (b r c)").partition_broadcast(P))
+            nc.sync.dma_start(out=x1[:], in_=extri1.rearrange("b r c -> (b r c)").partition_broadcast(P))
+            nc.sync.dma_start(out=x2[:], in_=extri2.rearrange("b r c -> (b r c)").partition_broadcast(P))
+            diff = const.tile([P, B, 3], F32, name="diff")
+            diff_sq = const.tile([P, B, 3], F32, name="diff_sq")
+            norm_sq = const.tile([P, B], F32, name="norm_sq")
+            baseline = const.tile([P, B], F32, name="baseline")
+            t1 = x1[:].rearrange("p (b r c) -> p b r c", r=4, c=4)[:, :, 0:3, 3]
+            t2 = x2[:].rearrange("p (b r c) -> p b r c", r=4, c=4)[:, :, 0:3, 3]
+            fx = k1[:].rearrange("p (b e) -> p b e", e=9)[:, :, 0]
+
+            def norm():
+                nc.vector.tensor_reduce(out=norm_sq[:], in_=diff_sq[:], axis=AX.X, op=ALU.add)
+                nc.gpsimd.tensor_tensor(out=baseline[:], in0=norm_sq[:], in1=half[:], op=ALU.pow)
+
+            return [
+                lambda: nc.vector.tensor_tensor(out=diff[:], in0=t1, in1=t2, op=ALU.subtract),
+                lambda: nc.vector.tensor_tensor(out=diff_sq[:], in0=diff[:], in1=diff[:], op=ALU.mult),
+                norm,
+                lambda: None,
+                lambda: None,
+                lambda: nc.vector.tensor_tensor(out=focal_base[:], in0=baseline[:], in1=fx, op=ALU.mult),
+            ]
+
+        def finish_steps(b):
+            rows = slice(b * H, (b + 1) * H)
+            cols = H * TILES
+            low = fin_pool.tile([P, H, TILES - 1], F32, name="low")
+            low_arg = fin_pool.tile([P, H, TILES - 1], F32, name="low_arg")
+            low_e = fin_pool.tile([P, H, TILES - 1], F32, name="low_e")
+            inv_sum = fin_pool.tile([P, H, TILES], F32, name="inv_sum")
+            corresp = fin_pool.tile([P, H, TILES], F32, name="corresp")
+            shift = fin_pool.tile([P, H, TILES], F32, name="shift")
+            disp_pos = fin_pool.tile([P, H, TILES], F32, name="disp_pos")
+            disp = fin_pool.tile([P, H, TILES], F32, name="disp")
+            inv_disp = fin_pool.tile([P, H, TILES], F32, name="inv_disp")
+            result = fin_pool.tile([P, 2, H, TILES], F32, name="result")
+            result_t = fin_pool.tile([P, P], F32, name="result_t")
+            flat = "p h i -> p (h i)"
+
+            def low_max(i):
+                nc.vector.tensor_reduce(
+                    out=low[:, :, i - 1], in_=block_max[:, rows, i, 0:i], axis=AX.X, op=ALU.max
+                )
+
+            def low_exp():
+                nc.vector.scalar_tensor_tensor(
+                    out=low_arg[:], in0=low[:], scalar=SCALE, in1=bias[:, rows, 1:TILES], op0=ALU.mult, op1=ALU.add
+                )
+                nc.scalar.activation(out=low_e[:], in_=low_arg[:], func=ACT.Exp)
+
+            def store():
+                nc.vector.tensor_tensor(out=result[:, 1], in0=e_max[:, rows, :], in1=inv_sum[:], op=ALU.mult)
+                turned = psum_const.tile([P, P], F32, name="turned")
+                nc.tensor.transpose(turned[:], result[:].rearrange("p o h i -> p (o h i)"), ident[:])
+                nc.scalar.copy(out=result_t[:], in_=turned[:])
+                for o, out in enumerate((out_0, out_1)):
+                    nc.sync.dma_start(
+                        out=out[b, 0].rearrange("h (i p) -> (h i) p", p=P),
+                        in_=result_t[o * cols : (o + 1) * cols, :],
+                    )
+
+            return [
+                lambda: low_max(1),
+                lambda: low_max(2),
+                lambda: low_max(3),
+                lambda: nc.vector.reciprocal(out=inv_sum[:], in_=e_sum[:, rows, :]),
+                low_exp,
+                lambda: nc.vector.tensor_tensor(out=corresp[:], in0=idx_sum[:, rows, :], in1=inv_sum[:], op=ALU.mult),
+                lambda: nc.vector.tensor_tensor(out=shift[:], in0=corresp[:], in1=w1_table[:], op=ALU.subtract),
+                lambda: nc.vector.tensor_scalar(
+                    out=disp_pos[:], in0=shift[:], scalar1=1.0 / W, scalar2=DISP_CLAMP, op0=ALU.mult, op1=ALU.max
+                ),
+                lambda: nc.vector.scalar_tensor_tensor(
+                    out=disp[:].rearrange(flat),
+                    in0=shift[:].rearrange(flat),
+                    scalar=-1.0 / W,
+                    in1=disp_pos[:].rearrange(flat),
+                    op0=ALU.mult,
+                    op1=ALU.max,
+                ),
+                lambda: nc.vector.tensor_tensor(
+                    out=e_max[:, rows, 1:TILES], in0=e_max[:, rows, 1:TILES], in1=low_e[:], op=ALU.max
+                ),
+                lambda: nc.vector.reciprocal(out=inv_disp[:], in_=disp[:]),
+                lambda: nc.vector.tensor_scalar(
+                    out=result[:, 0], in0=inv_disp[:], scalar1=focal_base[:, b : b + 1], scalar2=None, op0=ALU.mult
+                ),
+                store,
+            ]
+
+        for n in range(4):
+            load(n)
+        make_identity(nc, ident[:])
+        nc.gpsimd.iota(
+            w_col[:], pattern=[[P, TILES], [0, P]], base=0, channel_multiplier=1, allow_small_or_imprecise_dtypes=True
+        )
+        for j in range(TILES):
+            nc.tensor.transpose(ramp[:, j * P : (j + 1) * P], w_col[:, j, :], ident[:])
+        nc.gpsimd.iota(
+            w1_table[:], pattern=[[0, H], [P, TILES]], base=0, channel_multiplier=1, allow_small_or_imprecise_dtypes=True
+        )
+        nc.gpsimd.memset(half[:], 0.5)
+
+        interleave("vector", 0, (0, 512))
+        interleave("scalar", 0, (512, 768))
+        interleave("vector", 0, (768, 1024))
+        quantize(0)
+        interleave("scalar", 1, SHARE_A)
+        interleave("vector", 1, SHARE_B)
+        interleave("gpsimd", 1, SHARE_G)
+        interleave("scalar", 2, SHARE_A)
+
+        for n in range(ROWS):
+            load(n + 4)
+            if n == 1:
+                camera = camera_steps()
+            if n == 3:
+                side_steps.extend(camera)
+            if n == H + 1:
+                side_steps.extend(finish_steps(0))
+            correlate(n, 0)
+            correlate(n, 1)
+            block_maxima(n, 0)
+            block_maxima(n, 1)
+            index_sum(n - 1, 1)
+            index_sum(n - 1, 2)
+            softmax_pair(n, 0)
+            quantize(n + 1)
+            interleave("scalar", n + 2, SHARE_B)
+            interleave("gpsimd", n + 2, SHARE_G)
+            correlate(n, 2)
+            correlate(n, 3)
+            block_maxima(n, 2)
+            block_maxima(n, 3)
+            index_sum(n - 1, 3)
+            softmax_pair(n, 2)
+            diagonal_max(n - 1)
+            index_sum(n, 0)
+            interleave("scalar", n + 3, SHARE_A)
+
+        last = ROWS - 1
+        index_sum(last, 1)
+        index_sum(last, 2)
+        index_sum(last, 3)
+        diagonal_max(last)
+        for step in finish_steps(B - 1):
+            step()

@@ -24,9 +24,9 @@ SCALE = 1.0 / math.sqrt(C)
 DISP_CLAMP = 0.1
 E_PITCH = W + P
 
-SHARE_A = (0, 320)
-SHARE_B = (320, 640)
-SHARE_G = (640, 1024)
+SPLIT = 672
+SHARE_S = (0, SPLIT)
+SHARE_G = (SPLIT, 2 * W)
 
 
 def tile_costvolume_kernel(tc, img1, img2, intri1, intri2, extri1, extri2, out_0, out_1):
@@ -34,9 +34,9 @@ def tile_costvolume_kernel(tc, img1, img2, intri1, intri2, extri1, extri2, out_0
     with ExitStack() as ctx:
         const = ctx.enter_context(tc.tile_pool(name="const", bufs=1))
         raw_pool = ctx.enter_context(tc.tile_pool(name="raw", bufs=4))
-        grouped_pool = ctx.enter_context(tc.tile_pool(name="grouped", bufs=3))
+        grouped_pool = ctx.enter_context(tc.tile_pool(name="grouped", bufs=2))
         code_pool = ctx.enter_context(tc.tile_pool(name="codes", bufs=3))
-        e_pool = ctx.enter_context(tc.tile_pool(name="e", bufs=3))
+        e_pool = ctx.enter_context(tc.tile_pool(name="e", bufs=4))
         prod_pool = ctx.enter_context(tc.tile_pool(name="prod", bufs=3))
         fin_pool = ctx.enter_context(tc.tile_pool(name="fin", bufs=2))
         vol_pool = ctx.enter_context(tc.psum_pool(name="vol", bufs=6))
@@ -58,10 +58,9 @@ def tile_costvolume_kernel(tc, img1, img2, intri1, intri2, extri1, extri2, out_0
         raws, groups, codes, scales, es, vols = {}, {}, {}, {}, {}, {}
         side_steps = []
 
-        def vec():
+        def side_step():
             if side_steps:
                 side_steps.pop(0)()
-            return nc.vector
 
         def load(n):
             if n >= ROWS:
@@ -97,7 +96,7 @@ def tile_costvolume_kernel(tc, img1, img2, intri1, intri2, extri1, extri2, out_0
                 return
             codes[n] = code_pool.tile([P, 2 * W], U32, name="code", align_bytes=64)
             scales[n] = code_pool.tile([P, 2 * W], U8, name="scale", align_bytes=64)
-            vec().quantize_mx(
+            nc.vector.quantize_mx(
                 out=codes[n][:].bitcast(E5M2X4),
                 scales=scales[n][:],
                 in_=groups[n][:].rearrange("p w t -> p (w t)"),
@@ -116,7 +115,7 @@ def tile_costvolume_kernel(tc, img1, img2, intri1, intri2, extri1, extri2, out_0
             )
 
         def block_maxima(n, i):
-            vec().tensor_reduce(
+            nc.vector.tensor_reduce(
                 out=block_max[:, n, i, :],
                 in_=vols[n, i][:].rearrange("p (j c) -> p j c", c=P),
                 axis=AX.X,
@@ -126,13 +125,16 @@ def tile_costvolume_kernel(tc, img1, img2, intri1, intri2, extri1, extri2, out_0
         def diagonals(n, first, count):
             return es[n][:].rearrange("p (i c) -> p i c", c=E_PITCH)[:, first : first + count, 0:P]
 
-        def softmax_pair(n, first):
-            pair = slice(first, first + 2)
-            vec().tensor_reduce(out=row_max[:, n, pair], in_=block_max[:, n, pair, :], axis=AX.X, op=ALU.max)
-            nc.scalar.activation(out=bias[:, n, pair], in_=row_max[:, n, pair], func=ACT.Copy, scale=-SCALE)
+        def row_maximum(n):
+            nc.vector.tensor_reduce(out=row_max[:, n, :], in_=block_max[:, n], axis=AX.X, op=ALU.max)
+
+        def exp_bias(n):
+            nc.vector.tensor_scalar(out=bias[:, n, :], in0=row_max[:, n, :], scalar1=-SCALE, scalar2=None, op0=ALU.mult)
+
+        def exp_and_mask(n, first, count):
             if n not in es:
                 es[n] = e_pool.tile([P, TILES * E_PITCH], F32, name="e")
-            for i in (first, first + 1):
+            for i in range(first, first + count):
                 nc.scalar.activation(
                     out=es[n][:, i * W : (i + 1) * W],
                     in_=vols[n, i][:],
@@ -142,9 +144,9 @@ def tile_costvolume_kernel(tc, img1, img2, intri1, intri2, extri1, extri2, out_0
                     accum_out=e_sum[:, n, i : i + 1],
                 )
             nc.gpsimd.affine_select(
-                out=diagonals(n, first, 2),
-                in_=diagonals(n, first, 2),
-                pattern=[[0, 2], [-1, P]],
+                out=diagonals(n, first, count),
+                in_=diagonals(n, first, count),
+                pattern=[[0, count], [-1, P]],
                 compare_op=ALU.is_ge,
                 fill=0.0,
                 base=0,
@@ -156,7 +158,7 @@ def tile_costvolume_kernel(tc, img1, img2, intri1, intri2, extri1, extri2, out_0
                 return
             width = (i + 1) * P
             prod = prod_pool.tile([P, W], F32, name="prod")
-            vec().scalar_tensor_tensor(
+            nc.vector.scalar_tensor_tensor(
                 out=prod[:, 0:width],
                 in0=es[n][:, i * W : i * W + width],
                 scalar=1.0,
@@ -166,10 +168,10 @@ def tile_costvolume_kernel(tc, img1, img2, intri1, intri2, extri1, extri2, out_0
                 accum_out=idx_sum[:, n, i : i + 1],
             )
 
-        def diagonal_max(n):
-            if n < 0:
-                return
-            vec().tensor_reduce(out=e_max[:, n, :], in_=diagonals(n, 0, TILES), axis=AX.X, op=ALU.max)
+        def diagonal_max(n, first, count):
+            nc.vector.tensor_reduce(
+                out=e_max[:, n, first : first + count], in_=diagonals(n, first, count), axis=AX.X, op=ALU.max
+            )
 
         focal_base = const.tile([P, B], F32, name="focal_base")
 
@@ -196,7 +198,6 @@ def tile_costvolume_kernel(tc, img1, img2, intri1, intri2, extri1, extri2, out_0
                 lambda: nc.vector.tensor_tensor(out=diff[:], in0=t1, in1=t2, op=ALU.subtract),
                 lambda: nc.vector.tensor_tensor(out=diff_sq[:], in0=diff[:], in1=diff[:], op=ALU.mult),
                 norm,
-                lambda: None,
                 lambda: None,
                 lambda: nc.vector.tensor_tensor(out=focal_base[:], in0=baseline[:], in1=fx, op=ALU.mult),
             ]
@@ -285,43 +286,55 @@ def tile_costvolume_kernel(tc, img1, img2, intri1, intri2, extri1, extri2, out_0
         interleave("scalar", 0, (512, 768))
         interleave("vector", 0, (768, 1024))
         quantize(0)
-        interleave("scalar", 1, SHARE_A)
-        interleave("vector", 1, SHARE_B)
-        interleave("gpsimd", 1, SHARE_G)
-        interleave("scalar", 2, SHARE_A)
+        interleave("vector", 1, (0, 2 * W))
+        interleave("scalar", 2, SHARE_S)
 
+        last = ROWS - 1
+        mid = (SPLIT + 2 * W) // 2
         for n in range(ROWS):
             load(n + 4)
             if n == 1:
                 camera = camera_steps()
             if n == 3:
                 side_steps.extend(camera)
-            if n == H + 1:
+            if n == H + 2:
                 side_steps.extend(finish_steps(0))
-            correlate(n, 0)
-            correlate(n, 1)
-            block_maxima(n, 0)
-            block_maxima(n, 1)
-            index_sum(n - 1, 1)
-            index_sum(n - 1, 2)
-            softmax_pair(n, 0)
+            for i in range(TILES):
+                correlate(n, i)
+                block_maxima(n, i)
+            if n == 0:
+                interleave("vector", 2, (SPLIT, mid))
+            index_sum(n - 2, 3)
+            row_maximum(n)
+            side_step()
+            if n == 0:
+                interleave("vector", 2, (mid, 2 * W))
+            else:
+                diagonal_max(n - 1, 0, TILES)
+            exp_bias(n)
+            side_step()
             quantize(n + 1)
-            interleave("scalar", n + 2, SHARE_B)
-            interleave("gpsimd", n + 2, SHARE_G)
-            correlate(n, 2)
-            correlate(n, 3)
-            block_maxima(n, 2)
-            block_maxima(n, 3)
-            index_sum(n - 1, 3)
-            softmax_pair(n, 2)
-            diagonal_max(n - 1)
-            index_sum(n, 0)
-            interleave("scalar", n + 3, SHARE_A)
+            interleave("gpsimd", n + 3, SHARE_G)
+            if n < last:
+                exp_and_mask(n, 0, TILES)
+            else:
+                exp_and_mask(n, 2, 2)
+                exp_and_mask(n, 0, 2)
+            interleave("scalar", n + 3, SHARE_S)
+            for i in range(3):
+                index_sum(n - 1, i)
 
-        last = ROWS - 1
-        index_sum(last, 1)
-        index_sum(last, 2)
+        closing = finish_steps(B - 1)
+        index_sum(last - 1, 3)
+        for step in closing[:3]:
+            step()
         index_sum(last, 3)
-        diagonal_max(last)
-        for step in finish_steps(B - 1):
+        index_sum(last, 2)
+        diagonal_max(last, 2, 2)
+        closing[4]()
+        closing[3]()
+        index_sum(last, 1)
+        index_sum(last, 0)
+        diagonal_max(last, 0, 2)
+        for step in closing[5:]:
             step()

@@ -24,7 +24,7 @@ SCALE = 1.0 / math.sqrt(C)
 DISP_CLAMP = 0.1
 E_PITCH = W + P
 
-SPLIT = 672
+SPLIT = 560
 SHARE_S = (0, SPLIT)
 SHARE_G = (SPLIT, 2 * W)
 
@@ -36,8 +36,8 @@ def tile_costvolume_kernel(tc, img1, img2, intri1, intri2, extri1, extri2, out_0
         raw_pool = ctx.enter_context(tc.tile_pool(name="raw", bufs=4))
         grouped_pool = ctx.enter_context(tc.tile_pool(name="grouped", bufs=2))
         code_pool = ctx.enter_context(tc.tile_pool(name="codes", bufs=3))
-        e_pool = ctx.enter_context(tc.tile_pool(name="e", bufs=4))
-        prod_pool = ctx.enter_context(tc.tile_pool(name="prod", bufs=3))
+        e_pool = ctx.enter_context(tc.tile_pool(name="e", bufs=5))
+        prod_pool = ctx.enter_context(tc.tile_pool(name="prod", bufs=4))
         fin_pool = ctx.enter_context(tc.tile_pool(name="fin", bufs=2))
         vol_pool = ctx.enter_context(tc.psum_pool(name="vol", bufs=6))
         psum_const = ctx.enter_context(tc.psum_pool(name="psum_const", bufs=1))
@@ -46,16 +46,17 @@ def tile_costvolume_kernel(tc, img1, img2, intri1, intri2, extri1, extri2, out_0
         block_max = const.tile([P, ROWS, TILES, TILES], F32, name="block_max")
         row_max = const.tile([P, ROWS, TILES], F32, name="row_max")
         bias = const.tile([P, ROWS, TILES], F32, name="bias")
-        e_sum = const.tile([P, ROWS, TILES], F32, name="e_sum")
+        part_sum = const.tile([P, 2, ROWS, TILES], F32, name="part_sum")
         idx_sum = const.tile([P, ROWS, TILES], F32, name="idx_sum")
         e_max = const.tile([P, ROWS, TILES], F32, name="e_max")
         ident = const.tile([P, P], F32, name="ident")
         w_col = const.tile([P, TILES, P], F32, name="w_col")
-        w1_table = const.tile([P, H, TILES], F32, name="w1_table")
+        part_weight = const.tile([P, 2, H, TILES], F32, name="part_weight")
+        fold_weight = const.tile([P, W], F32, name="fold_weight")
         half = const.tile([P, B], F32, name="half")
         ramp = psum_const.tile([P, W], F32, name="ramp")
 
-        raws, groups, codes, scales, es, vols = {}, {}, {}, {}, {}, {}
+        raws, groups, codes, scales, es, vols, folds = {}, {}, {}, {}, {}, {}, {}
         side_steps = []
 
         def side_step():
@@ -102,7 +103,28 @@ def tile_costvolume_kernel(tc, img1, img2, intri1, intri2, extri1, extri2, out_0
                 in_=groups[n][:].rearrange("p w t -> p (w t)"),
             )
 
+        def folded(n, i):
+            return 0 <= n < ROWS - 2 and (i == 3 or (i == 2 and n % 4 != 3))
+
+        def fold(n):
+            tiles = [i for i in range(TILES) if folded(n, i)]
+            if not tiles:
+                return
+            folds[n] = psum_const.tile([P, 2, W // 2], F32, name="fold", tag="spare")
+            for i in tiles:
+                span = (i + 1) * P // 2
+                for a in range(2):
+                    nc.tensor.matmul(
+                        out=folds[n][:, i - 2, 0:span],
+                        lhsT=ident[:],
+                        rhs=es[n][:, i * W + a * span : i * W + (a + 1) * span],
+                        start=(a == 0),
+                        stop=(a == 1),
+                    )
+
         def correlate(n, i):
+            if n >= ROWS:
+                return
             vols[n, i] = vol_pool.tile([P, W], F32, name="vol")
             nc.tensor.matmul_mx(
                 out=vols[n, i][:],
@@ -135,14 +157,17 @@ def tile_costvolume_kernel(tc, img1, img2, intri1, intri2, extri1, extri2, out_0
             if n not in es:
                 es[n] = e_pool.tile([P, TILES * E_PITCH], F32, name="e")
             for i in range(first, first + count):
-                nc.scalar.activation(
-                    out=es[n][:, i * W : (i + 1) * W],
-                    in_=vols[n, i][:],
-                    func=ACT.Exp,
-                    scale=SCALE,
-                    bias=bias[:, n, i : i + 1],
-                    accum_out=e_sum[:, n, i : i + 1],
-                )
+                span = (i + 1) * P // 2
+                parts = [(0, 0, span), (1, span, W)] if folded(n, i) else [(1, 0, W)]
+                for a, lo, hi in parts:
+                    nc.scalar.activation(
+                        out=es[n][:, i * W + lo : i * W + hi],
+                        in_=vols[n, i][:, lo:hi],
+                        func=ACT.Exp,
+                        scale=SCALE,
+                        bias=bias[:, n, i : i + 1],
+                        accum_out=part_sum[:, a, n, i : i + 1],
+                    )
             nc.gpsimd.affine_select(
                 out=diagonals(n, first, count),
                 in_=diagonals(n, first, count),
@@ -156,13 +181,18 @@ def tile_costvolume_kernel(tc, img1, img2, intri1, intri2, extri1, extri2, out_0
         def index_sum(n, i):
             if n < 0:
                 return
-            width = (i + 1) * P
+            if folded(n, i):
+                width = (i + 1) * P // 2
+                values, weights = folds[n][:, i - 2, 0:width], fold_weight[:, width : 2 * width]
+            else:
+                width = (i + 1) * P
+                values, weights = es[n][:, i * W : i * W + width], ramp[:, 0:width]
             prod = prod_pool.tile([P, W], F32, name="prod")
             nc.vector.scalar_tensor_tensor(
                 out=prod[:, 0:width],
-                in0=es[n][:, i * W : i * W + width],
+                in0=values,
                 scalar=1.0,
-                in1=ramp[:, 0:width],
+                in1=weights,
                 op0=ALU.mult,
                 op1=ALU.mult,
                 accum_out=idx_sum[:, n, i : i + 1],
@@ -209,7 +239,10 @@ def tile_costvolume_kernel(tc, img1, img2, intri1, intri2, extri1, extri2, out_0
             low_arg = fin_pool.tile([P, H, TILES - 1], F32, name="low_arg")
             low_e = fin_pool.tile([P, H, TILES - 1], F32, name="low_e")
             inv_sum = fin_pool.tile([P, H, TILES], F32, name="inv_sum")
-            corresp = fin_pool.tile([P, H, TILES], F32, name="corresp")
+            e_sum = fin_pool.tile([P, H, TILES], F32, name="e_sum")
+            weighted = fin_pool.tile([P, 2, H, TILES], F32, name="weighted")
+            offset = fin_pool.tile([P, H, TILES], F32, name="offset")
+            excess = fin_pool.tile([P, H, TILES], F32, name="excess")
             shift = fin_pool.tile([P, H, TILES], F32, name="shift")
             disp_pos = fin_pool.tile([P, H, TILES], F32, name="disp_pos")
             disp = fin_pool.tile([P, H, TILES], F32, name="disp")
@@ -230,8 +263,7 @@ def tile_costvolume_kernel(tc, img1, img2, intri1, intri2, extri1, extri2, out_0
                 nc.scalar.activation(out=low_e[:], in_=low_arg[:], func=ACT.Exp)
 
             def store():
-                nc.vector.tensor_tensor(out=result[:, 1], in0=e_max[:, rows, :], in1=inv_sum[:], op=ALU.mult)
-                turned = psum_const.tile([P, P], F32, name="turned")
+                turned = psum_const.tile([P, P], F32, name="turned", tag="spare")
                 nc.tensor.transpose(turned[:], result[:].rearrange("p o h i -> p (o h i)"), ident[:])
                 nc.scalar.copy(out=result_t[:], in_=turned[:])
                 for o, out in enumerate((out_0, out_1)):
@@ -240,14 +272,24 @@ def tile_costvolume_kernel(tc, img1, img2, intri1, intri2, extri1, extri2, out_0
                         in_=result_t[o * cols : (o + 1) * cols, :],
                     )
 
-            return [
-                lambda: low_max(1),
-                lambda: low_max(2),
-                lambda: low_max(3),
-                lambda: nc.vector.reciprocal(out=inv_sum[:], in_=e_sum[:, rows, :]),
-                low_exp,
-                lambda: nc.vector.tensor_tensor(out=corresp[:], in0=idx_sum[:, rows, :], in1=inv_sum[:], op=ALU.mult),
-                lambda: nc.vector.tensor_tensor(out=shift[:], in0=corresp[:], in1=w1_table[:], op=ALU.subtract),
+            before_exp = [lambda: low_max(1), lambda: low_max(2), lambda: low_max(3), low_exp]
+            after_exp = [
+                lambda: nc.vector.tensor_tensor(
+                    out=e_sum[:], in0=part_sum[:, 0, rows, :], in1=part_sum[:, 1, rows, :], op=ALU.add
+                ),
+                lambda: nc.vector.tensor_tensor(
+                    out=weighted[:], in0=part_sum[:, :, rows, :], in1=part_weight[:], op=ALU.mult
+                ),
+                lambda: nc.vector.reciprocal(out=inv_sum[:], in_=e_sum[:]),
+                lambda: nc.vector.tensor_tensor(out=offset[:], in0=weighted[:, 0], in1=weighted[:, 1], op=ALU.add),
+            ]
+            after_sums = [
+                lambda: nc.vector.tensor_tensor(out=excess[:], in0=idx_sum[:, rows, :], in1=offset[:], op=ALU.subtract),
+                lambda: nc.vector.tensor_tensor(
+                    out=e_max[:, rows, 1:TILES], in0=e_max[:, rows, 1:TILES], in1=low_e[:], op=ALU.max
+                ),
+                lambda: nc.vector.tensor_tensor(out=shift[:], in0=excess[:], in1=inv_sum[:], op=ALU.mult),
+                lambda: nc.vector.tensor_tensor(out=result[:, 1], in0=e_max[:, rows, :], in1=inv_sum[:], op=ALU.mult),
                 lambda: nc.vector.tensor_scalar(
                     out=disp_pos[:], in0=shift[:], scalar1=1.0 / W, scalar2=DISP_CLAMP, op0=ALU.mult, op1=ALU.max
                 ),
@@ -259,15 +301,12 @@ def tile_costvolume_kernel(tc, img1, img2, intri1, intri2, extri1, extri2, out_0
                     op0=ALU.mult,
                     op1=ALU.max,
                 ),
-                lambda: nc.vector.tensor_tensor(
-                    out=e_max[:, rows, 1:TILES], in0=e_max[:, rows, 1:TILES], in1=low_e[:], op=ALU.max
-                ),
                 lambda: nc.vector.reciprocal(out=inv_disp[:], in_=disp[:]),
                 lambda: nc.vector.tensor_scalar(
                     out=result[:, 0], in0=inv_disp[:], scalar1=focal_base[:, b : b + 1], scalar2=None, op0=ALU.mult
                 ),
-                store,
             ]
+            return before_exp, after_exp, after_sums, store
 
         for n in range(4):
             load(n)
@@ -277,8 +316,17 @@ def tile_costvolume_kernel(tc, img1, img2, intri1, intri2, extri1, extri2, out_0
         )
         for j in range(TILES):
             nc.tensor.transpose(ramp[:, j * P : (j + 1) * P], w_col[:, j, :], ident[:])
+        nc.gpsimd.memset(part_sum[:, 0], 0.0)
+        for a, (base, step) in enumerate(((P // 2, P + P // 2), (0, P))):
+            nc.gpsimd.iota(
+                part_weight[:, a],
+                pattern=[[0, H], [step, TILES]],
+                base=base,
+                channel_multiplier=1,
+                allow_small_or_imprecise_dtypes=True,
+            )
         nc.gpsimd.iota(
-            w1_table[:], pattern=[[0, H], [P, TILES]], base=0, channel_multiplier=1, allow_small_or_imprecise_dtypes=True
+            fold_weight[:], pattern=[[1, W]], base=0, channel_multiplier=0, allow_small_or_imprecise_dtypes=True
         )
         nc.gpsimd.memset(half[:], 0.5)
 
@@ -286,6 +334,8 @@ def tile_costvolume_kernel(tc, img1, img2, intri1, intri2, extri1, extri2, out_0
         interleave("scalar", 0, (512, 768))
         interleave("vector", 0, (768, 1024))
         quantize(0)
+        for i in range(TILES):
+            correlate(0, i)
         interleave("vector", 1, (0, 2 * W))
         interleave("scalar", 2, SHARE_S)
 
@@ -298,19 +348,19 @@ def tile_costvolume_kernel(tc, img1, img2, intri1, intri2, extri1, extri2, out_0
             if n == 3:
                 side_steps.extend(camera)
             if n == H + 2:
-                side_steps.extend(finish_steps(0))
+                before_exp, after_exp, after_sums, store_first = finish_steps(0)
+                side_steps.extend(before_exp + after_exp + after_sums)
             for i in range(TILES):
-                correlate(n, i)
                 block_maxima(n, i)
             if n == 0:
                 interleave("vector", 2, (SPLIT, mid))
-            index_sum(n - 2, 3)
+            index_sum(n - 2, 1)
             row_maximum(n)
             side_step()
             if n == 0:
                 interleave("vector", 2, (mid, 2 * W))
-            else:
-                diagonal_max(n - 1, 0, TILES)
+            if n >= 2:
+                diagonal_max(n - 2, 0, TILES)
             exp_bias(n)
             side_step()
             quantize(n + 1)
@@ -321,20 +371,30 @@ def tile_costvolume_kernel(tc, img1, img2, intri1, intri2, extri1, extri2, out_0
                 exp_and_mask(n, 2, 2)
                 exp_and_mask(n, 0, 2)
             interleave("scalar", n + 3, SHARE_S)
-            for i in range(3):
-                index_sum(n - 1, i)
+            for i in range(TILES):
+                correlate(n + 1, i)
+            index_sum(n - 1, 0)
+            index_sum(n - 2, 2)
+            index_sum(n - 2, 3)
+            if n == last - 3:
+                assert not side_steps
+                store_first()
+            fold(n - 1)
 
-        closing = finish_steps(B - 1)
-        index_sum(last - 1, 3)
-        for step in closing[:3]:
+        before_exp, after_exp, after_sums, store_last = finish_steps(B - 1)
+        for i in range(1, TILES):
+            index_sum(last - 1, i)
+        diagonal_max(last - 1, 0, TILES)
+        for step in before_exp:
             step()
         index_sum(last, 3)
         index_sum(last, 2)
         diagonal_max(last, 2, 2)
-        closing[4]()
-        closing[3]()
+        for step in after_exp:
+            step()
         index_sum(last, 1)
         index_sum(last, 0)
         diagonal_max(last, 0, 2)
-        for step in closing[5:]:
+        for step in after_sums:
             step()
+        store_last()

@@ -24,9 +24,8 @@ SCALE = 1.0 / math.sqrt(C)
 DISP_CLAMP = 0.1
 E_PITCH = W + P
 
-SPLIT = 560
-SHARE_S = (0, SPLIT)
-SHARE_G = (SPLIT, 2 * W)
+SHARE_S = (0, 512)
+SHARE_G = (512, 2 * W)
 
 
 def tile_costvolume_kernel(tc, img1, img2, intri1, intri2, extri1, extri2, out_0, out_1):
@@ -104,7 +103,7 @@ def tile_costvolume_kernel(tc, img1, img2, intri1, intri2, extri1, extri2, out_0
             )
 
         def folded(n, i):
-            return 0 <= n < ROWS - 2 and (i == 3 or (i == 2 and n % 4 != 3))
+            return 0 <= n < ROWS - 1 and (i == 3 or (i == 2 and n % 4 != 3))
 
         def fold(n):
             tiles = [i for i in range(TILES) if folded(n, i)]
@@ -331,16 +330,15 @@ def tile_costvolume_kernel(tc, img1, img2, intri1, intri2, extri1, extri2, out_0
         nc.gpsimd.memset(half[:], 0.5)
 
         interleave("vector", 0, (0, 512))
-        interleave("scalar", 0, (512, 768))
-        interleave("vector", 0, (768, 1024))
+        interleave("scalar", 0, (512, 672))
+        interleave("vector", 0, (672, 1024))
         quantize(0)
         for i in range(TILES):
             correlate(0, i)
         interleave("vector", 1, (0, 2 * W))
-        interleave("scalar", 2, SHARE_S)
+        interleave("scalar", 2, (0, 768))
 
         last = ROWS - 1
-        mid = (SPLIT + 2 * W) // 2
         for n in range(ROWS):
             load(n + 4)
             if n == 1:
@@ -353,12 +351,12 @@ def tile_costvolume_kernel(tc, img1, img2, intri1, intri2, extri1, extri2, out_0
             for i in range(TILES):
                 block_maxima(n, i)
             if n == 0:
-                interleave("vector", 2, (SPLIT, mid))
+                interleave("vector", 2, (768, 896))
             index_sum(n - 2, 1)
             row_maximum(n)
             side_step()
             if n == 0:
-                interleave("vector", 2, (mid, 2 * W))
+                interleave("vector", 2, (896, 1024))
             if n >= 2:
                 diagonal_max(n - 2, 0, TILES)
             exp_bias(n)
@@ -382,14 +380,15 @@ def tile_costvolume_kernel(tc, img1, img2, intri1, intri2, extri1, extri2, out_0
             fold(n - 1)
 
         before_exp, after_exp, after_sums, store_last = finish_steps(B - 1)
-        for i in range(1, TILES):
-            index_sum(last - 1, i)
+        index_sum(last - 1, 1)
         diagonal_max(last - 1, 0, TILES)
         for step in before_exp:
             step()
         index_sum(last, 3)
         index_sum(last, 2)
         diagonal_max(last, 2, 2)
+        index_sum(last - 1, 2)
+        index_sum(last - 1, 3)
         for step in after_exp:
             step()
         index_sum(last, 1)

@@ -19,27 +19,41 @@ AX = mybir.AxisListType
 P = 128
 PACK = 4
 ROWS = B * H
+LAST = ROWS - 1
 TILES = W // P
 SCALE = 1.0 / math.sqrt(C)
 DISP_CLAMP = 0.1
-E_PITCH = W + P
+DIAG_PITCH = W + P
 
-SHARE_S = (0, 512)
-SHARE_G = (512, 2 * W)
+COPY_SPLIT = 536
+SCALAR_SHARE = (0, COPY_SPLIT)
+GPSIMD_SHARE = (COPY_SPLIT, 2 * W)
+FIRST_ROW_SPLIT = 672
+
+LOAD_AHEAD = 4
+COPY_AHEAD = 3
+SUM_BEHIND = 2
+CAMERA_LOAD_ROW = 1
+CAMERA_ROW = 3
+FIRST_STORE_ROW = ROWS - COPY_AHEAD
+
+
+def folded(n, i):
+    return 0 <= n < LAST and (i == 3 or (i == 2 and n % 4 != 3))
 
 
 def tile_costvolume_kernel(tc, img1, img2, intri1, intri2, extri1, extri2, out_0, out_1):
     nc = tc.nc
     with ExitStack() as ctx:
         const = ctx.enter_context(tc.tile_pool(name="const", bufs=1))
-        raw_pool = ctx.enter_context(tc.tile_pool(name="raw", bufs=4))
+        raw_pool = ctx.enter_context(tc.tile_pool(name="raw", bufs=LOAD_AHEAD))
         grouped_pool = ctx.enter_context(tc.tile_pool(name="grouped", bufs=2))
         code_pool = ctx.enter_context(tc.tile_pool(name="codes", bufs=3))
         e_pool = ctx.enter_context(tc.tile_pool(name="e", bufs=5))
-        prod_pool = ctx.enter_context(tc.tile_pool(name="prod", bufs=4))
-        fin_pool = ctx.enter_context(tc.tile_pool(name="fin", bufs=2))
+        prod_pool = ctx.enter_context(tc.tile_pool(name="prod", bufs=TILES))
+        fin_pool = ctx.enter_context(tc.tile_pool(name="fin", bufs=B))
         vol_pool = ctx.enter_context(tc.psum_pool(name="vol", bufs=6))
-        psum_const = ctx.enter_context(tc.psum_pool(name="psum_const", bufs=1))
+        psum_single = ctx.enter_context(tc.psum_pool(name="psum_single", bufs=1))
         ctx.enter_context(tc.manual_schedule())
 
         block_max = const.tile([P, ROWS, TILES, TILES], F32, name="block_max")
@@ -53,7 +67,7 @@ def tile_costvolume_kernel(tc, img1, img2, intri1, intri2, extri1, extri2, out_0
         part_weight = const.tile([P, 2, H, TILES], F32, name="part_weight")
         fold_weight = const.tile([P, W], F32, name="fold_weight")
         half = const.tile([P, B], F32, name="half")
-        ramp = psum_const.tile([P, W], F32, name="ramp")
+        ramp = psum_single.tile([P, W], F32, name="ramp")
 
         raws, groups, codes, scales, es, vols, folds = {}, {}, {}, {}, {}, {}, {}
         side_steps = []
@@ -67,10 +81,10 @@ def tile_costvolume_kernel(tc, img1, img2, intri1, intri2, extri1, extri2, out_0
                 return
             b, h = divmod(n, H)
             raws[n] = raw_pool.tile([P, PACK, 2 * W], BF16, name="raw")
-            for k, img in enumerate((img1, img2)):
+            for side, img in enumerate((img1, img2)):
                 nc.sync.dma_start(
-                    out=raws[n][:, :, k * W : (k + 1) * W],
-                    in_=img[b, :, h, :].rearrange("(p j) w -> p j w", j=PACK),
+                    out=raws[n][:, :, side * W : (side + 1) * W],
+                    in_=img[b, :, h, :].rearrange("(p t) w -> p t w", t=PACK),
                 )
 
         def interleave(engine, n, share):
@@ -102,14 +116,11 @@ def tile_costvolume_kernel(tc, img1, img2, intri1, intri2, extri1, extri2, out_0
                 in_=groups[n][:].rearrange("p w t -> p (w t)"),
             )
 
-        def folded(n, i):
-            return 0 <= n < ROWS - 1 and (i == 3 or (i == 2 and n % 4 != 3))
-
         def fold(n):
             tiles = [i for i in range(TILES) if folded(n, i)]
             if not tiles:
                 return
-            folds[n] = psum_const.tile([P, 2, W // 2], F32, name="fold", tag="spare")
+            folds[n] = psum_single.tile([P, 2, W // 2], F32, name="fold", tag="spare")
             for i in tiles:
                 span = (i + 1) * P // 2
                 for a in range(2):
@@ -144,7 +155,7 @@ def tile_costvolume_kernel(tc, img1, img2, intri1, intri2, extri1, extri2, out_0
             )
 
         def diagonals(n, first, count):
-            return es[n][:].rearrange("p (i c) -> p i c", c=E_PITCH)[:, first : first + count, 0:P]
+            return es[n][:].rearrange("p (i c) -> p i c", c=DIAG_PITCH)[:, first : first + count, 0:P]
 
         def row_maximum(n):
             nc.vector.tensor_reduce(out=row_max[:, n, :], in_=block_max[:, n], axis=AX.X, op=ALU.max)
@@ -154,7 +165,7 @@ def tile_costvolume_kernel(tc, img1, img2, intri1, intri2, extri1, extri2, out_0
 
         def exp_and_mask(n, first, count):
             if n not in es:
-                es[n] = e_pool.tile([P, TILES * E_PITCH], F32, name="e")
+                es[n] = e_pool.tile([P, TILES * DIAG_PITCH], F32, name="e")
             for i in range(first, first + count):
                 span = (i + 1) * P // 2
                 parts = [(0, 0, span), (1, span, W)] if folded(n, i) else [(1, 0, W)]
@@ -223,15 +234,14 @@ def tile_costvolume_kernel(tc, img1, img2, intri1, intri2, extri1, extri2, out_0
                 nc.vector.tensor_reduce(out=norm_sq[:], in_=diff_sq[:], axis=AX.X, op=ALU.add)
                 nc.gpsimd.tensor_tensor(out=baseline[:], in0=norm_sq[:], in1=half[:], op=ALU.pow)
 
-            return [
+            first_steps = [
                 lambda: nc.vector.tensor_tensor(out=diff[:], in0=t1, in1=t2, op=ALU.subtract),
                 lambda: nc.vector.tensor_tensor(out=diff_sq[:], in0=diff[:], in1=diff[:], op=ALU.mult),
                 norm,
-                lambda: None,
-                lambda: nc.vector.tensor_tensor(out=focal_base[:], in0=baseline[:], in1=fx, op=ALU.mult),
             ]
+            return first_steps, lambda: nc.vector.tensor_tensor(out=focal_base[:], in0=baseline[:], in1=fx, op=ALU.mult)
 
-        def finish_steps(b):
+        def closing_steps(b):
             rows = slice(b * H, (b + 1) * H)
             cols = H * TILES
             low = fin_pool.tile([P, H, TILES - 1], F32, name="low")
@@ -262,7 +272,7 @@ def tile_costvolume_kernel(tc, img1, img2, intri1, intri2, extri1, extri2, out_0
                 nc.scalar.activation(out=low_e[:], in_=low_arg[:], func=ACT.Exp)
 
             def store():
-                turned = psum_const.tile([P, P], F32, name="turned", tag="spare")
+                turned = psum_single.tile([P, P], F32, name="turned", tag="spare")
                 nc.tensor.transpose(turned[:], result[:].rearrange("p o h i -> p (o h i)"), ident[:])
                 nc.scalar.copy(out=result_t[:], in_=turned[:])
                 for o, out in enumerate((out_0, out_1)):
@@ -271,7 +281,7 @@ def tile_costvolume_kernel(tc, img1, img2, intri1, intri2, extri1, extri2, out_0
                         in_=result_t[o * cols : (o + 1) * cols, :],
                     )
 
-            before_exp = [lambda: low_max(1), lambda: low_max(2), lambda: low_max(3), low_exp]
+            after_max = [lambda: low_max(1), lambda: low_max(2), lambda: low_max(3), low_exp]
             after_exp = [
                 lambda: nc.vector.tensor_tensor(
                     out=e_sum[:], in0=part_sum[:, 0, rows, :], in1=part_sum[:, 1, rows, :], op=ALU.add
@@ -305,9 +315,9 @@ def tile_costvolume_kernel(tc, img1, img2, intri1, intri2, extri1, extri2, out_0
                     out=result[:, 0], in0=inv_disp[:], scalar1=focal_base[:, b : b + 1], scalar2=None, op0=ALU.mult
                 ),
             ]
-            return before_exp, after_exp, after_sums, store
+            return after_max, after_exp, after_sums, store
 
-        for n in range(4):
+        for n in range(LOAD_AHEAD):
             load(n)
         make_identity(nc, ident[:])
         nc.gpsimd.iota(
@@ -329,71 +339,68 @@ def tile_costvolume_kernel(tc, img1, img2, intri1, intri2, extri1, extri2, out_0
         )
         nc.gpsimd.memset(half[:], 0.5)
 
-        interleave("vector", 0, (0, 512))
-        interleave("scalar", 0, (512, 672))
-        interleave("vector", 0, (672, 1024))
+        interleave("vector", 0, (0, W))
+        interleave("scalar", 0, (W, FIRST_ROW_SPLIT))
+        interleave("vector", 0, (FIRST_ROW_SPLIT, 2 * W))
         quantize(0)
         for i in range(TILES):
             correlate(0, i)
         interleave("vector", 1, (0, 2 * W))
-        interleave("scalar", 2, (0, 768))
+        interleave("scalar", 2, (0, 2 * W))
 
-        last = ROWS - 1
         for n in range(ROWS):
-            load(n + 4)
-            if n == 1:
-                camera = camera_steps()
-            if n == 3:
-                side_steps.extend(camera)
-            if n == H + 2:
-                before_exp, after_exp, after_sums, store_first = finish_steps(0)
-                side_steps.extend(before_exp + after_exp + after_sums)
+            load(n + LOAD_AHEAD)
+            if n == CAMERA_LOAD_ROW:
+                camera_first, camera_last = camera_steps()
+            if n == CAMERA_ROW:
+                side_steps.extend(camera_first)
+            if n == H + SUM_BEHIND:
+                after_max, after_exp, after_sums, store_first = closing_steps(0)
+                side_steps.extend([camera_last] + after_max + after_exp + after_sums)
             for i in range(TILES):
                 block_maxima(n, i)
-            if n == 0:
-                interleave("vector", 2, (768, 896))
-            index_sum(n - 2, 1)
+            if n >= SUM_BEHIND:
+                diagonal_max(n - SUM_BEHIND, 0, TILES)
             row_maximum(n)
             side_step()
-            if n == 0:
-                interleave("vector", 2, (896, 1024))
-            if n >= 2:
-                diagonal_max(n - 2, 0, TILES)
+            quantize(n + 1)
             exp_bias(n)
             side_step()
-            quantize(n + 1)
-            interleave("gpsimd", n + 3, SHARE_G)
-            if n < last:
+            if n == 0:
+                interleave("vector", COPY_AHEAD, SCALAR_SHARE)
+            interleave("gpsimd", n + COPY_AHEAD, GPSIMD_SHARE)
+            if n < LAST:
                 exp_and_mask(n, 0, TILES)
             else:
                 exp_and_mask(n, 2, 2)
                 exp_and_mask(n, 0, 2)
-            interleave("scalar", n + 3, SHARE_S)
+            if n > 0:
+                interleave("scalar", n + COPY_AHEAD, SCALAR_SHARE)
             for i in range(TILES):
                 correlate(n + 1, i)
-            index_sum(n - 1, 0)
-            index_sum(n - 2, 2)
-            index_sum(n - 2, 3)
-            if n == last - 3:
+            for i in range(TILES):
+                index_sum(n - SUM_BEHIND, i)
+            if n == FIRST_STORE_ROW:
                 assert not side_steps
                 store_first()
             fold(n - 1)
 
-        before_exp, after_exp, after_sums, store_last = finish_steps(B - 1)
-        index_sum(last - 1, 1)
-        diagonal_max(last - 1, 0, TILES)
-        for step in before_exp:
+        after_max, after_exp, after_sums, store_last = closing_steps(B - 1)
+        index_sum(LAST - 1, 0)
+        index_sum(LAST - 1, 1)
+        diagonal_max(LAST - 1, 0, TILES)
+        for step in after_max:
             step()
-        index_sum(last, 3)
-        index_sum(last, 2)
-        diagonal_max(last, 2, 2)
-        index_sum(last - 1, 2)
-        index_sum(last - 1, 3)
+        index_sum(LAST, 3)
+        index_sum(LAST, 2)
+        diagonal_max(LAST, 2, 2)
+        index_sum(LAST - 1, 2)
+        index_sum(LAST - 1, 3)
         for step in after_exp:
             step()
-        index_sum(last, 1)
-        index_sum(last, 0)
-        diagonal_max(last, 0, 2)
+        index_sum(LAST, 1)
+        index_sum(LAST, 0)
+        diagonal_max(LAST, 0, 2)
         for step in after_sums:
             step()
         store_last()

import math
from contextlib import ExitStack

import concourse.mybir as mybir
from concourse.masks import make_identity

B, C, H, W = 2, 512, 16, 512
FLOPS = 2 * B * H * W * W * C

F32 = mybir.dt.float32
BF16 = mybir.dt.bfloat16
U32 = mybir.dt.uint32
U8 = mybir.dt.uint8
E5M2X4 = mybir.dt.float8_e5m2_x4
ALU = mybir.AluOpType
ACT = mybir.ActivationFunctionType
AX = mybir.AxisListType

P = 128
PACK = 4
ROWS = B * H
LAST = ROWS - 1
TILES = W // P
SCALE = 1.0 / math.sqrt(C)
DISP_CLAMP = 0.1
DIAG_PITCH = W + P

COPY_SPLIT = 536
SCALAR_SHARE = (0, COPY_SPLIT)
GPSIMD_SHARE = (COPY_SPLIT, 2 * W)
FIRST_ROW_SPLIT = 672

LOAD_AHEAD = 4
COPY_AHEAD = 3
SUM_BEHIND = 2
CAMERA_LOAD_ROW = 1
CAMERA_ROW = 3
FIRST_STORE_ROW = ROWS - COPY_AHEAD


def folded(n, i):
    return 0 <= n < LAST and (i == 3 or (i == 2 and n % 4 != 3))


def tile_costvolume_kernel(tc, img1, img2, intri1, intri2, extri1, extri2, out_0, out_1):
    nc = tc.nc
    with ExitStack() as ctx:
        const = ctx.enter_context(tc.tile_pool(name="const", bufs=1))
        raw_pool = ctx.enter_context(tc.tile_pool(name="raw", bufs=LOAD_AHEAD))
        grouped_pool = ctx.enter_context(tc.tile_pool(name="grouped", bufs=2))
        code_pool = ctx.enter_context(tc.tile_pool(name="codes", bufs=3))
        e_pool = ctx.enter_context(tc.tile_pool(name="e", bufs=5))
        prod_pool = ctx.enter_context(tc.tile_pool(name="prod", bufs=TILES))
        fin_pool = ctx.enter_context(tc.tile_pool(name="fin", bufs=B))
        vol_pool = ctx.enter_context(tc.psum_pool(name="vol", bufs=6))
        psum_single = ctx.enter_context(tc.psum_pool(name="psum_single", bufs=1))
        ctx.enter_context(tc.manual_schedule())

        block_max = const.tile([P, ROWS, TILES, TILES], F32, name="block_max")
        row_max = const.tile([P, ROWS, TILES], F32, name="row_max")
        bias = const.tile([P, ROWS, TILES], F32, name="bias")
        part_sum = const.tile([P, 2, ROWS, TILES], F32, name="part_sum")
        idx_sum = const.tile([P, ROWS, TILES], F32, name="idx_sum")
        e_max = const.tile([P, ROWS, TILES], F32, name="e_max")
        ident = const.tile([P, P], F32, name="ident")
        w_col = const.tile([P, TILES, P], F32, name="w_col")
        part_weight = const.tile([P, 2, H, TILES], F32, name="part_weight")
        fold_weight = const.tile([P, W], F32, name="fold_weight")
        half = const.tile([P, B], F32, name="half")
        ramp = psum_single.tile([P, W], F32, name="ramp")

        raws, groups, codes, scales, es, vols, folds = {}, {}, {}, {}, {}, {}, {}
        side_steps = []

        def side_step():
            if side_steps:
                side_steps.pop(0)()

        def load(n):
            if n >= ROWS:
                return
            b, h = divmod(n, H)
            raws[n] = raw_pool.tile([P, PACK, 2 * W], BF16, name="raw")
            for side, img in enumerate((img1, img2)):
                nc.sync.dma_start(
                    out=raws[n][:, :, side * W : (side + 1) * W],
                    in_=img[b, :, h, :].rearrange("(p t) w -> p t w", t=PACK),
                )

        def interleave(engine, n, share):
            if n >= ROWS:
                return
            if n not in groups:
                groups[n] = grouped_pool.tile([P, 2 * W, PACK], BF16, name="grouped", align_bytes=64)
            lo, hi = share
            dst = groups[n][:, lo:hi, :]
            src = raws[n][:, :, lo:hi]
            if engine == "gpsimd":
                nc.gpsimd.tensor_copy(out=dst, in_=src.rearrange("p t w -> p w t"))
                return
            dst = dst.rearrange("p (c i) t -> p c t i", i=4)
            src = src.rearrange("p t (c i) -> p c t i", i=4)
            if engine == "scalar":
                nc.scalar.copy(out=dst, in_=src)
            else:
                nc.vector.tensor_copy(out=dst, in_=src)

        def quantize(n):
            if n >= ROWS:
                return
            codes[n] = code_pool.tile([P, 2 * W], U32, name="code", align_bytes=64)
            scales[n] = code_pool.tile([P, 2 * W], U8, name="scale", align_bytes=64)
            nc.vector.quantize_mx(
                out=codes[n][:].bitcast(E5M2X4),
                scales=scales[n][:],
                in_=groups[n][:].rearrange("p w t -> p (w t)"),
            )

        def fold(n):
            tiles = [i for i in range(TILES) if folded(n, i)]
            if not tiles:
                return
            folds[n] = psum_single.tile([P, 2, W // 2], F32, name="fold", tag="spare")
            for i in tiles:
                span = (i + 1) * P // 2
                for a in range(2):
                    nc.tensor.matmul(
                        out=folds[n][:, i - 2, 0:span],
                        lhsT=ident[:],
                        rhs=es[n][:, i * W + a * span : i * W + (a + 1) * span],
                        start=(a == 0),
                        stop=(a == 1),
                    )

        def correlate(n, i):
            if n >= ROWS:
                return
            vols[n, i] = vol_pool.tile([P, W], F32, name="vol")
            nc.tensor.matmul_mx(
                out=vols[n, i][:],
                lhsT=codes[n][:, i * P : (i + 1) * P].bitcast(E5M2X4),
                lhsT_scale=scales[n][:, i * P : (i + 1) * P],
                rhs=codes[n][:, W : 2 * W].bitcast(E5M2X4),
                rhs_scale=scales[n][:, W : 2 * W],
                start=True,
                stop=True,
            )

        def block_maxima(n, i):
            nc.vector.tensor_reduce(
                out=block_max[:, n, i, :],
                in_=vols[n, i][:].rearrange("p (j c) -> p j c", c=P),
                axis=AX.X,
                op=ALU.max,
            )

        def diagonals(n, first, count):
            return es[n][:].rearrange("p (i c) -> p i c", c=DIAG_PITCH)[:, first : first + count, 0:P]

        def row_maximum(n):
            nc.vector.tensor_reduce(out=row_max[:, n, :], in_=block_max[:, n], axis=AX.X, op=ALU.max)

        def exp_bias(n):
            nc.vector.tensor_scalar(out=bias[:, n, :], in0=row_max[:, n, :], scalar1=-SCALE, scalar2=None, op0=ALU.mult)

        def exp_and_mask(n, first, count):
            if n not in es:
                es[n] = e_pool.tile([P, TILES * DIAG_PITCH], F32, name="e")
            for i in range(first, first + count):
                span = (i + 1) * P // 2
                parts = [(0, 0, span), (1, span, W)] if folded(n, i) else [(1, 0, W)]
                for a, lo, hi in parts:
                    nc.scalar.activation(
                        out=es[n][:, i * W + lo : i * W + hi],
                        in_=vols[n, i][:, lo:hi],
                        func=ACT.Exp,
                        scale=SCALE,
                        bias=bias[:, n, i : i + 1],
                        accum_out=part_sum[:, a, n, i : i + 1],
                    )
            nc.gpsimd.affine_select(
                out=diagonals(n, first, count),
                in_=diagonals(n, first, count),
                pattern=[[0, count], [-1, P]],
                compare_op=ALU.is_ge,
                fill=0.0,
                base=0,
                channel_multiplier=1,
            )

        def index_sum(n, i):
            if n < 0:
                return
            if folded(n, i):
                width = (i + 1) * P // 2
                values, weights = folds[n][:, i - 2, 0:width], fold_weight[:, width : 2 * width]
            else:
                width = (i + 1) * P
                values, weights = es[n][:, i * W : i * W + width], ramp[:, 0:width]
            prod = prod_pool.tile([P, W], F32, name="prod")
            nc.vector.scalar_tensor_tensor(
                out=prod[:, 0:width],
                in0=values,
                scalar=1.0,
                in1=weights,
                op0=ALU.mult,
                op1=ALU.mult,
                accum_out=idx_sum[:, n, i : i + 1],
            )

        def diagonal_max(n, first, count):
            nc.vector.tensor_reduce(
                out=e_max[:, n, first : first + count], in_=diagonals(n, first, count), axis=AX.X, op=ALU.max
            )

        focal_base = const.tile([P, B], F32, name="focal_base")

        def camera_steps():
            k1 = const.tile([P, B * 9], BF16, name="k1")
            x1 = const.tile([P, B * 16], BF16, name="x1")
            x2 = const.tile([P, B * 16], BF16, name="x2")
            nc.sync.dma_start(out=k1[:], in_=intri1.rearrange("b r c -> (b r c)").partition_broadcast(P))
            nc.sync.dma_start(out=x1[:], in_=extri1.rearrange("b r c -> (b r c)").partition_broadcast(P))
            nc.sync.dma_start(out=x2[:], in_=extri2.rearrange("b r c -> (b r c)").partition_broadcast(P))
            diff = const.tile([P, B, 3], F32, name="diff")
            diff_sq = const.tile([P, B, 3], F32, name="diff_sq")
            norm_sq = const.tile([P, B], F32, name="norm_sq")
            baseline = const.tile([P, B], F32, name="baseline")
            t1 = x1[:].rearrange("p (b r c) -> p b r c", r=4, c=4)[:, :, 0:3, 3]
            t2 = x2[:].rearrange("p (b r c) -> p b r c", r=4, c=4)[:, :, 0:3, 3]
            fx = k1[:].rearrange("p (b e) -> p b e", e=9)[:, :, 0]

            def norm():
                nc.vector.tensor_reduce(out=norm_sq[:], in_=diff_sq[:], axis=AX.X, op=ALU.add)
                nc.gpsimd.tensor_tensor(out=baseline[:], in0=norm_sq[:], in1=half[:], op=ALU.pow)

            first_steps = [
                lambda: nc.vector.tensor_tensor(out=diff[:], in0=t1, in1=t2, op=ALU.subtract),
                lambda: nc.vector.tensor_tensor(out=diff_sq[:], in0=diff[:], in1=diff[:], op=ALU.mult),
                norm,
            ]
            return first_steps, lambda: nc.vector.tensor_tensor(out=focal_base[:], in0=baseline[:], in1=fx, op=ALU.mult)

        def closing_steps(b):
            rows = slice(b * H, (b + 1) * H)
            cols = H * TILES
            low = fin_pool.tile([P, H, TILES - 1], F32, name="low")
            low_arg = fin_pool.tile([P, H, TILES - 1], F32, name="low_arg")
            low_e = fin_pool.tile([P, H, TILES - 1], F32, name="low_e")
            inv_sum = fin_pool.tile([P, H, TILES], F32, name="inv_sum")
            e_sum = fin_pool.tile([P, H, TILES], F32, name="e_sum")
            weighted = fin_pool.tile([P, 2, H, TILES], F32, name="weighted")
            offset = fin_pool.tile([P, H, TILES], F32, name="offset")
            excess = fin_pool.tile([P, H, TILES], F32, name="excess")
            shift = fin_pool.tile([P, H, TILES], F32, name="shift")
            disp_pos = fin_pool.tile([P, H, TILES], F32, name="disp_pos")
            disp = fin_pool.tile([P, H, TILES], F32, name="disp")
            inv_disp = fin_pool.tile([P, H, TILES], F32, name="inv_disp")
            result = fin_pool.tile([P, 2, H, TILES], F32, name="result")
            result_t = fin_pool.tile([P, P], F32, name="result_t")
            flat = "p h i -> p (h i)"

            def low_max(i):
                nc.vector.tensor_reduce(
                    out=low[:, :, i - 1], in_=block_max[:, rows, i, 0:i], axis=AX.X, op=ALU.max
                )

            def low_exp():
                nc.vector.scalar_tensor_tensor(
                    out=low_arg[:], in0=low[:], scalar=SCALE, in1=bias[:, rows, 1:TILES], op0=ALU.mult, op1=ALU.add
                )
                nc.scalar.activation(out=low_e[:], in_=low_arg[:], func=ACT.Exp)

            def store():
                turned = psum_single.tile([P, P], F32, name="turned", tag="spare")
                nc.tensor.transpose(turned[:], result[:].rearrange("p o h i -> p (o h i)"), ident[:])
                nc.scalar.copy(out=result_t[:], in_=turned[:])
                for o, out in enumerate((out_0, out_1)):
                    nc.sync.dma_start(
                        out=out[b, 0].rearrange("h (i p) -> (h i) p", p=P),
                        in_=result_t[o * cols : (o + 1) * cols, :],
                    )

            after_max = [lambda: low_max(1), lambda: low_max(2), lambda: low_max(3), low_exp]
            after_exp = [
                lambda: nc.vector.tensor_tensor(
                    out=e_sum[:], in0=part_sum[:, 0, rows, :], in1=part_sum[:, 1, rows, :], op=ALU.add
                ),
                lambda: nc.vector.tensor_tensor(
                    out=weighted[:], in0=part_sum[:, :, rows, :], in1=part_weight[:], op=ALU.mult
                ),
                lambda: nc.vector.reciprocal(out=inv_sum[:], in_=e_sum[:]),
                lambda: nc.vector.tensor_tensor(out=offset[:], in0=weighted[:, 0], in1=weighted[:, 1], op=ALU.add),
            ]
            after_sums = [
                lambda: nc.vector.tensor_tensor(out=excess[:], in0=idx_sum[:, rows, :], in1=offset[:], op=ALU.subtract),
                lambda: nc.vector.tensor_tensor(
                    out=e_max[:, rows, 1:TILES], in0=e_max[:, rows, 1:TILES], in1=low_e[:], op=ALU.max
                ),
                lambda: nc.vector.tensor_tensor(out=shift[:], in0=excess[:], in1=inv_sum[:], op=ALU.mult),
                lambda: nc.vector.tensor_tensor(out=result[:, 1], in0=e_max[:, rows, :], in1=inv_sum[:], op=ALU.mult),
                lambda: nc.vector.tensor_scalar(
                    out=disp_pos[:], in0=shift[:], scalar1=1.0 / W, scalar2=DISP_CLAMP, op0=ALU.mult, op1=ALU.max
                ),
                lambda: nc.vector.scalar_tensor_tensor(
                    out=disp[:].rearrange(flat),
                    in0=shift[:].rearrange(flat),
                    scalar=-1.0 / W,
                    in1=disp_pos[:].rearrange(flat),
                    op0=ALU.mult,
                    op1=ALU.max,
                ),
                lambda: nc.vector.reciprocal(out=inv_disp[:], in_=disp[:]),
                lambda: nc.vector.tensor_scalar(
                    out=result[:, 0], in0=inv_disp[:], scalar1=focal_base[:, b : b + 1], scalar2=None, op0=ALU.mult
                ),
            ]
            return after_max, after_exp, after_sums, store

        for n in range(LOAD_AHEAD):
            load(n)
        make_identity(nc, ident[:])
        nc.gpsimd.iota(
            w_col[:], pattern=[[P, TILES], [0, P]], base=0, channel_multiplier=1, allow_small_or_imprecise_dtypes=True
        )
        for j in range(TILES):
            nc.tensor.transpose(ramp[:, j * P : (j + 1) * P], w_col[:, j, :], ident[:])
        nc.gpsimd.memset(part_sum[:, 0], 0.0)
        for a, (base, step) in enumerate(((P // 2, P + P // 2), (0, P))):
            nc.gpsimd.iota(
                part_weight[:, a],
                pattern=[[0, H], [step, TILES]],
                base=base,
                channel_multiplier=1,
                allow_small_or_imprecise_dtypes=True,
            )
        nc.gpsimd.iota(
            fold_weight[:], pattern=[[1, W]], base=0, channel_multiplier=0, allow_small_or_imprecise_dtypes=True
        )
        nc.gpsimd.memset(half[:], 0.5)

        interleave("vector", 0, (0, W))
        interleave("scalar", 0, (W, FIRST_ROW_SPLIT))
        interleave("vector", 0, (FIRST_ROW_SPLIT, 2 * W))
        quantize(0)
        for i in range(TILES):
            correlate(0, i)
        interleave("vector", 1, (0, 2 * W))
        interleave("scalar", 2, (0, 2 * W))

        for n in range(ROWS):
            load(n + LOAD_AHEAD)
            if n == CAMERA_LOAD_ROW:
                camera_first, camera_last = camera_steps()
            if n == CAMERA_ROW:
                side_steps.extend(camera_first)
            if n == H + SUM_BEHIND:
                after_max, after_exp, after_sums, store_first = closing_steps(0)
                side_steps.extend([camera_last] + after_max + after_exp + after_sums)
            for i in range(TILES):
                block_maxima(n, i)
            if n >= SUM_BEHIND:
                diagonal_max(n - SUM_BEHIND, 0, TILES)
            row_maximum(n)
            side_step()
            quantize(n + 1)
            exp_bias(n)
            side_step()
            if n == 0:
                interleave("vector", COPY_AHEAD, SCALAR_SHARE)
            interleave("gpsimd", n + COPY_AHEAD, GPSIMD_SHARE)
            if n < LAST:
                exp_and_mask(n, 0, TILES)
            else:
                exp_and_mask(n, 2, 2)
                exp_and_mask(n, 0, 2)
            if n > 0:
                interleave("scalar", n + COPY_AHEAD, SCALAR_SHARE)
            for i in range(TILES):
                correlate(n + 1, i)
            for i in range(TILES):
                index_sum(n - SUM_BEHIND, i)
            if n == FIRST_STORE_ROW:
                assert not side_steps
                store_first()
            fold(n - 1)

        after_max, after_exp, after_sums, store_last = closing_steps(B - 1)
        index_sum(LAST - 1, 0)
        index_sum(LAST - 1, 1)
        diagonal_max(LAST - 1, 0, TILES)
        for step in after_max:
            step()
        index_sum(LAST, 3)
        index_sum(LAST, 2)
        diagonal_max(LAST, 2, 2)
        index_sum(LAST - 1, 2)
        index_sum(LAST - 1, 3)
        for step in after_exp:
            step()
        index_sum(LAST, 1)
        index_sum(LAST, 0)
        diagonal_max(LAST, 0, 2)
        for step in after_sums:
            step()
        store_last()
